import numpy as np
import ml_dtypes


def mxq(x, axis, fmt="e4m3"):
    dtype, down = {"e4m3": (ml_dtypes.float8_e4m3fn, 7), "e5m2": (ml_dtypes.float8_e5m2, 14)}[fmt]
    v = np.moveaxis(np.asarray(x, np.float32).astype(ml_dtypes.bfloat16).astype(np.float64), axis, -1)
    blocks = v.reshape(v.shape[:-1] + (-1, 32))
    amax = np.abs(blocks).max(-1, keepdims=True)
    byte = np.maximum(np.where(amax > 0, np.frexp(amax)[1] - 1 + 127, 0) - down, 1)
    scale = np.exp2(byte - 127.0)
    codes = (blocks / scale).astype(np.float32).astype(dtype).astype(np.float64)
    return np.moveaxis((codes * scale).reshape(v.shape), -1, axis)


WIDE = False


def mx_kscale(k):
    if not WIDE:
        return np.ones(k)
    levels = np.array([10, -10, 5, -5, 0])
    if k % 512:
        return np.exp2(np.random.permutation(np.resize(levels, k // 32))).repeat(32)
    a = np.empty((k // 512, 16))
    for p in range(k // 512):
        a[p, :8] = np.random.permutation(np.resize(levels, 8))
        for g in range(8):
            far = levels[np.abs(levels - a[p, g]) >= 10]
            a[p, g + 8] = far[np.random.randint(len(far))]
    return np.exp2(a.ravel()).repeat(32)


BF16 = ml_dtypes.bfloat16


def bf(x):
    return np.asarray(x, np.float32).astype(BF16)


def f64(x):
    return np.asarray(x).astype(np.float64)


B, C_IN, C_OUT, H, W = 2, 1024, 768, 32, 32
P = 4
G = P * P


def setup_inputs():
    s = mx_kscale(C_IN)
    bound = np.sqrt(6.0 / (C_IN + C_OUT))
    return {"x": bf(np.random.standard_normal((B, C_IN, H, W)) * s[None, :, None, None]),
            "Wg": bf(np.random.uniform(-bound, bound, (G, C_OUT, C_IN)) / s[None, None, :]),
            "bg": bf(np.random.standard_normal((G, C_OUT)) * 0.25)}


def reference(x, Wg, bg):
    Bb, C, Hh, Ww = x.shape
    H4, W4 = Hh // P, Ww // P
    xq = mxq(f64(x), 1, "e4m3")
    wq = mxq(f64(Wg), 2, "e4m3")
    xg = xq.reshape(Bb, C, H4, P, W4, P).transpose(0, 2, 4, 3, 5, 1)
    xg = xg.reshape(Bb * H4 * W4, G, C).transpose(1, 0, 2)
    y = xg @ wq.transpose(0, 2, 1)
    O = y.shape[-1]
    y = y.transpose(1, 0, 2).reshape(Bb, H4, W4, G, O) + f64(bg)
    y = y.reshape(Bb, H4, W4, P, P, O).transpose(0, 5, 1, 3, 2, 4)
    return y.reshape(Bb, O, Hh, Ww)

@@ -1,0 +1,247 @@
+from contextlib import ExitStack
+
+import concourse.mybir as mybir
+from concourse.masks import make_identity
+
+F32 = mybir.dt.float32
+BF16 = mybir.dt.bfloat16
+U32 = mybir.dt.uint32
+U8 = mybir.dt.uint8
+FP8X4 = mybir.dt.float8_e4m3fn_x4
+
+FLOPS = 2 * 16 * 128 * 1024 * 768
+
+P = 128
+LOOK = 3
+RAW_BUFS = 9
+RAW_COLS = 5120
+PHASES = (5, 1)
+
+
+def tile_groupwiselinearprojector_kernel(tc, x, Wg, bg, out):
+    nc = tc.nc
+    with ExitStack() as ctx:
+        keep = ctx.enter_context(tc.tile_pool(name="keep", bufs=1))
+        rawp = ctx.enter_context(tc.tile_pool(name="rawp", bufs=RAW_BUFS))
+        grpp = ctx.enter_context(tc.tile_pool(name="grpp", bufs=5))
+        codp = ctx.enter_context(tc.tile_pool(name="codp", bufs=16))
+        tps = ctx.enter_context(tc.psum_pool(name="tps", bufs=6))
+        pos = ctx.enter_context(tc.psum_pool(name="pos", bufs=2))
+        ctx.enter_context(tc.manual_schedule())
+
+        ident = keep.tile([P, P], F32, name="ident")
+        make_identity(nc, ident[:])
+
+        bgpad = keep.tile([P, 768], BF16, name="bgpad")
+        nc.vector.memset(bgpad[:], 0.0)
+        nc.scalar.dma_start(out=bgpad[0:16, :], in_=bg)
+
+        tiles = []
+        j0 = 0
+        for nj in PHASES:
+            if nj > 1:
+                for g in range(16):
+                    tiles.append([(g, j0 + a) for a in range(nj)])
+            else:
+                for g in range(0, 16, 2):
+                    tiles.append([(g, j0), (g + 1, j0)])
+            j0 += nj
+        stream = [(m, g, j, a * 512) for m, units in enumerate(tiles) for a, (g, j) in enumerate(units)]
+        pairs = [(stream[n], stream[n + 1]) for n in range(0, len(stream), 2)]
+        n_pairs = len(pairs)
+        where = {}
+        last_pair = [0] * len(tiles)
+        for i, units in enumerate(pairs):
+            for m, g, j, off in units:
+                where[(g, j)] = i
+                last_pair[m] = i
+        order = sorted([(max([where[(4 * pr + q, j)] for q in range(4)]), j, pr) for pr in range(4) for j in range(6)])
+        slots = []
+        for av, j, pr in order:
+            slots.append(max(av, slots[-1] + 2) if slots else av)
+        lim = n_pairs - 1
+        for n in reversed(range(len(order))):
+            if slots[n] > lim:
+                slots[n] = max(order[n][0], lim)
+            lim = min(lim, slots[n]) - 1
+        sched = [[] for k in range(n_pairs)]
+        for n, (av, j, pr) in enumerate(order):
+            sched[slots[n]].append((pr, j))
+
+        raw = {}
+
+        def load_w(m):
+            units = tiles[m]
+            t = rawp.tile([P, RAW_COLS], BF16, name="wr%d" % m, tag="raw", align_bytes=64)
+            g, j = units[0]
+            if units[1][0] == g:
+                nj = len(units)
+                nc.sync.dma_start(
+                    out=t[:, 0 : nj * 1024],
+                    in_=Wg[g].rearrange("(q j) k -> q (j k)", j=6)[:, j * 1024 : (j + nj) * 1024],
+                )
+            else:
+                nc.sync.dma_start(
+                    out=t[:, 0:2048].rearrange("p (g k) -> p g k", g=2),
+                    in_=Wg[g : g + 2].rearrange("g (q j) k -> q g j k", j=6)[:, :, j, :],
+                )
+            raw[m] = t
+
+        chunks = ((0, 0), (1, 0), (0, 1), (1, 1))
+        xr = {}
+        for b, c in chunks:
+            t = rawp.tile([P, RAW_COLS], BF16, name="xr%d%d" % (b, c), tag="raw", align_bytes=64)
+            nc.sync.dma_start(
+                out=t[:, 0:4096],
+                in_=x[b, 512 * c : 512 * c + 512].rearrange("(p t) h w -> p (t h w)", t=4),
+            )
+            xr[(b, c)] = t
+
+        xc = keep.tile([P, 4096], U32, name="xc", align_bytes=64)
+        xs = keep.tile([P, 4096], U8, name="xs", align_bytes=64)
+        gx = {}
+
+        def regroup(b, c):
+            for pr in range(4):
+                src = (
+                    xr[(b, c)][:, 0:4096]
+                    .rearrange("p (a r n) -> p r a n", a=32, r=4, n=32)[:, pr]
+                    .rearrange("p (t h) (w q) -> p q h w t", t=4, q=4)
+                )
+                lo = (pr % 2) * 2048
+                dst = (
+                    gx[(c, pr // 2)][:, lo : lo + 2048]
+                    .rearrange("p (q b n) -> p q b n", q=4, b=2)[:, :, b]
+                    .rearrange("p q (h w t) -> p q h w t", h=8, w=8, t=4)
+                )
+                if pr < 3:
+                    nc.vector.tensor_copy(out=dst, in_=src)
+                else:
+                    for q in range(4):
+                        nc.scalar.copy(out=dst[:, q], in_=src[:, q])
+
+        def quant_x(c, gh):
+            base = (c * 16 + gh * 8) * P
+            nc.vector.quantize_mx(
+                out=xc[:, base : base + 1024].bitcast(FP8X4),
+                scales=xs[:, base : base + 1024],
+                in_=gx[(c, gh)][:, 0:4096],
+            )
+
+        bgf = keep.tile([P, 768], F32, name="bgf")
+        bias = keep.tile([P, 96], F32, name="bias")
+
+        def x_stage():
+            for c in range(2):
+                for gh in range(2):
+                    gx[(c, gh)] = rawp.tile([P, RAW_COLS], BF16, name="gx%d%d" % (c, gh), tag="raw", align_bytes=64)
+            regroup(0, 0)
+            regroup(1, 0)
+            regroup(0, 1)
+            quant_x(0, 0)
+            quant_x(0, 1)
+            regroup(1, 1)
+            quant_x(1, 0)
+            quant_x(1, 1)
+            nc.vector.tensor_copy(
+                out=bgf[:].rearrange("g (j q) -> g j q", j=6),
+                in_=bgpad[:].rearrange("g (q j) -> g j q", j=6),
+            )
+
+        def spread_bias():
+            for js in ((0, 1, 2, 3), (4, 5)):
+                tb = tps.tile([P, 512], F32, name="tb%d" % js[0], tag="tp")
+                for n, j in enumerate(js):
+                    nc.tensor.transpose(tb[:, n * P : (n + 1) * P], bgf[:, j * P : (j + 1) * P], ident[:])
+                nc.scalar.copy(
+                    out=bias[:, js[0] * 16 : (js[-1] + 1) * 16].rearrange("p (j g) -> p j g", g=16),
+                    in_=tb[:, 0 : len(js) * P].rearrange("p (j g) -> p j g", g=P)[:, :, 0:16],
+                )
+
+        ot = [keep.tile([P, 2048], F32, name="ot%d" % j) for j in range(6)]
+        grp = {}
+        codes = {}
+
+        def transpose_pair(i):
+            units = pairs[i]
+            gt = grpp.tile([P, 2048], BF16, name="grp%d" % i, tag="grp", align_bytes=64)
+            g32 = gt[:].bitcast(F32)
+            banks = []
+            for n, (m, g, j, off) in enumerate(units):
+                words = raw[m][:].bitcast(F32)
+                tp = tps.tile([P, 512], F32, name="tp%d_%d" % (i, n), tag="tp")
+                for c in range(2):
+                    for u in range(2):
+                        s = 2 * c + u
+                        lo = off + 2 * P * c
+                        nc.tensor.transpose(tp[:, s * P : (s + 1) * P], words[:, lo + u : lo + 2 * P : 2], ident[:])
+                banks.append(tp)
+            for n, tp in enumerate(banks):
+                nc.scalar.copy(
+                    out=g32[:, n * 512 : (n + 1) * 512].rearrange("p (c o u) -> p c o u", c=2, o=P, u=2),
+                    in_=tp[:].rearrange("p (c u o) -> p c o u", c=2, u=2, o=P),
+                )
+            grp[i] = gt
+
+        def quant_pair(i):
+            wc = codp.tile([P, 512], U32, name="wc%d" % i, tag="wc", align_bytes=64)
+            ws = codp.tile([P, 512], U8, name="ws%d" % i, tag="ws", align_bytes=64)
+            nc.vector.quantize_mx(out=wc[:].bitcast(FP8X4), scales=ws[:], in_=grp[i][:])
+            for n, (m, g, j, off) in enumerate(pairs[i]):
+                codes[(g, j)] = (wc, ws, n)
+
+        def multiply(pr, j):
+            po = pos.tile([P, 512], F32, name="po%d_%d" % (pr, j), tag="po")
+            for q in range(4):
+                g = 4 * pr + q
+                wc, ws, n = codes[(g, j)]
+                for c in range(2):
+                    wl = (2 * n + c) * P
+                    xl = (16 * c + g) * P
+                    nc.tensor.matmul_mx(
+                        out=po[:, q * P : (q + 1) * P],
+                        lhsT=wc[:, wl : wl + P].bitcast(FP8X4),
+                        lhsT_scale=ws[:, wl : wl + P],
+                        rhs=xc[:, xl : xl + P].bitcast(FP8X4),
+                        rhs_scale=xs[:, xl : xl + P],
+                        start=(c == 0),
+                        stop=(c == 1),
+                    )
+            return po
+
+        def add_bias(pr, j, po):
+            lo = 16 * j + 4 * pr
+            nc.vector.tensor_tensor(
+                out=ot[j][:].rearrange("p (a r n) -> p r a n", a=16, r=4, n=32)[:, pr].rearrange("p a (w q) -> p a w q", q=4),
+                in0=po[:].rearrange("p (q a w) -> p a w q", q=4, a=16, w=8),
+                in1=bias[:, lo : lo + 4].unsqueeze(1).unsqueeze(1).to_broadcast([P, 16, 8, 4]),
+                op=mybir.AluOpType.add,
+            )
+            done[j] += 1
+            if done[j] == 4:
+                nc.sync.dma_start(
+                    out=out.rearrange("b (q j) h w -> j q b (h w)", j=6)[j],
+                    in_=ot[j][:].rearrange("p (b n) -> p b n", b=2),
+                )
+
+        done = [0] * 6
+        x_stage()
+        next_m = 0
+        pending = []
+        for i in range(n_pairs + LOOK + 1):
+            while next_m < len(tiles) and (next_m < RAW_BUFS or last_pair[next_m - RAW_BUFS] < i):
+                load_w(next_m)
+                next_m += 1
+            if i == 8:
+                spread_bias()
+            if i < n_pairs:
+                transpose_pair(i)
+            k = i - LOOK
+            if 0 <= k < n_pairs:
+                quant_pair(k)
+            for pr, j, po in pending:
+                add_bias(pr, j, po)
+            pending = []
+            if 0 <= k < n_pairs:
+                for pr, j in sched[k]:
+                    pending.append((pr, j, multiply(pr, j)))

@@ -25,6 +25,7 @@ def tile_groupwiselinearprojector_kernel(tc, x, Wg, bg, out):
         rawp = ctx.enter_context(tc.tile_pool(name="rawp", bufs=RAW_BUFS))
         grpp = ctx.enter_context(tc.tile_pool(name="grpp", bufs=5))
         codp = ctx.enter_context(tc.tile_pool(name="codp", bufs=16))
+        srtp = ctx.enter_context(tc.tile_pool(name="srtp", bufs=3))
         tps = ctx.enter_context(tc.psum_pool(name="tps", bufs=6))
         pos = ctx.enter_context(tc.psum_pool(name="pos", bufs=2))
         ctx.enter_context(tc.manual_schedule())
@@ -162,19 +163,40 @@ def tile_groupwiselinearprojector_kernel(tc, x, Wg, bg, out):
         grp = {}
         codes = {}
 
+        sorted_words = {}
+
+        def sort_pair(i):
+            st = srtp.tile([P, 2048], BF16, name="srt%d" % i, tag="srt", align_bytes=64)
+            units = pairs[i]
+            dst = st[:].bitcast(F32)
+            spans = [(units[0], 2)] if units[0][0] == units[1][0] and units[0][3] + 512 == units[1][3] else [(units[0], 1), (units[1], 1)]
+            at = 0
+            for (m, g, j, off), cnt in spans:
+                n = cnt * 512
+                nc.vector.tensor_copy(
+                    out=dst[:, at : at + n].rearrange("p (c u w) -> p c u w", u=2, w=P),
+                    in_=raw[m][:].bitcast(F32)[:, off : off + n].rearrange("p (c w u) -> p c u w", u=2, w=P),
+                )
+                at += n
+            sorted_words[i] = dst
+
         def transpose_pair(i):
             units = pairs[i]
             gt = grpp.tile([P, 2048], BF16, name="grp%d" % i, tag="grp", align_bytes=64)
             g32 = gt[:].bitcast(F32)
             banks = []
             for n, (m, g, j, off) in enumerate(units):
-                words = raw[m][:].bitcast(F32)
+                if i in sorted_words:
+                    words, off = sorted_words[i], n * 512
+                else:
+                    words = raw[m][:].bitcast(F32)
                 tp = tps.tile([P, 512], F32, name="tp%d_%d" % (i, n), tag="tp")
                 for c in range(2):
                     for u in range(2):
                         s = 2 * c + u
                         lo = off + 2 * P * c
-                        nc.tensor.transpose(tp[:, s * P : (s + 1) * P], words[:, lo + u : lo + 2 * P : 2], ident[:])
+                        src = words[:, lo + u * P : lo + (u + 1) * P] if i in sorted_words else words[:, lo + u : lo + 2 * P : 2]
+                        nc.tensor.transpose(tp[:, s * P : (s + 1) * P], src, ident[:])
                 banks.append(tp)
             for n, tp in enumerate(banks):
                 nc.scalar.copy(
@@ -226,6 +248,9 @@ def tile_groupwiselinearprojector_kernel(tc, x, Wg, bg, out):
 
         done = [0] * 6
         x_stage()
+        def is_sorted(i):
+            return i % 2 == 0
+
         next_m = 0
         pending = []
         for i in range(n_pairs + LOOK + 1):
@@ -237,6 +262,8 @@ def tile_groupwiselinearprojector_kernel(tc, x, Wg, bg, out):
             if i < n_pairs:
                 transpose_pair(i)
             k = i - LOOK
+            if i + 2 < n_pairs and is_sorted(i + 2):
+                sort_pair(i + 2)
             if 0 <= k < n_pairs:
                 quant_pair(k)
             for pr, j, po in pending:

@@ -13,9 +13,10 @@ FLOPS = 2 * 16 * 128 * 1024 * 768
 
 P = 128
 LOOK = 3
-RAW_BUFS = 9
-RAW_COLS = 5120
-PHASES = (5, 1)
+RAW_BUFS = 14
+RAW_COLS = 4096
+NJ = 3
+SPACING = 2
 
 
 def tile_groupwiselinearprojector_kernel(tc, x, Wg, bg, out):
@@ -24,8 +25,9 @@ def tile_groupwiselinearprojector_kernel(tc, x, Wg, bg, out):
         keep = ctx.enter_context(tc.tile_pool(name="keep", bufs=1))
         rawp = ctx.enter_context(tc.tile_pool(name="rawp", bufs=RAW_BUFS))
         grpp = ctx.enter_context(tc.tile_pool(name="grpp", bufs=5))
-        codp = ctx.enter_context(tc.tile_pool(name="codp", bufs=16))
-        srtp = ctx.enter_context(tc.tile_pool(name="srtp", bufs=3))
+        codp = ctx.enter_context(tc.tile_pool(name="codp", bufs=11))
+        srtp = ctx.enter_context(tc.tile_pool(name="srtp", bufs=2))
+        outp = ctx.enter_context(tc.tile_pool(name="outp", bufs=4))
         tps = ctx.enter_context(tc.psum_pool(name="tps", bufs=6))
         pos = ctx.enter_context(tc.psum_pool(name="pos", bufs=2))
         ctx.enter_context(tc.manual_schedule())
@@ -37,17 +39,15 @@ def tile_groupwiselinearprojector_kernel(tc, x, Wg, bg, out):
         nc.vector.memset(bgpad[:], 0.0)
         nc.scalar.dma_start(out=bgpad[0:16, :], in_=bg)
 
-        tiles = []
-        j0 = 0
-        for nj in PHASES:
-            if nj > 1:
-                for g in range(16):
-                    tiles.append([(g, j0 + a) for a in range(nj)])
-            else:
-                for g in range(0, 16, 2):
-                    tiles.append([(g, j0), (g + 1, j0)])
-            j0 += nj
-        stream = [(m, g, j, a * 512) for m, units in enumerate(tiles) for a, (g, j) in enumerate(units)]
+        tiles = [(g, 0) for g in range(16)] + [(g, NJ) for g in range(16)]
+
+        def unit(g, j):
+            return (g + 16 * (j // NJ), g, j, (j % NJ) * 512)
+
+        stream = [unit(g, j) for g in range(16) for j in (0, 1, 2)]
+        stream += [unit(g, j) for g in range(8) for j in (3, 4, 5)]
+        stream += [unit(g, j) for g in range(8, 16) for j in (3, 4)]
+        stream += [unit(g, 5) for g in range(8, 16)]
         pairs = [(stream[n], stream[n + 1]) for n in range(0, len(stream), 2)]
         n_pairs = len(pairs)
         where = {}
@@ -55,11 +55,11 @@ def tile_groupwiselinearprojector_kernel(tc, x, Wg, bg, out):
         for i, units in enumerate(pairs):
             for m, g, j, off in units:
                 where[(g, j)] = i
-                last_pair[m] = i
+                last_pair[m] = max(last_pair[m], i)
         order = sorted([(max([where[(4 * pr + q, j)] for q in range(4)]), j, pr) for pr in range(4) for j in range(6)])
         slots = []
         for av, j, pr in order:
-            slots.append(max(av, slots[-1] + 2) if slots else av)
+            slots.append(max(av, slots[-1] + SPACING) if slots else av)
         lim = n_pairs - 1
         for n in reversed(range(len(order))):
             if slots[n] > lim:
@@ -72,20 +72,12 @@ def tile_groupwiselinearprojector_kernel(tc, x, Wg, bg, out):
         raw = {}
 
         def load_w(m):
-            units = tiles[m]
+            g, j = tiles[m]
             t = rawp.tile([P, RAW_COLS], BF16, name="wr%d" % m, tag="raw", align_bytes=64)
-            g, j = units[0]
-            if units[1][0] == g:
-                nj = len(units)
-                nc.sync.dma_start(
-                    out=t[:, 0 : nj * 1024],
-                    in_=Wg[g].rearrange("(q j) k -> q (j k)", j=6)[:, j * 1024 : (j + nj) * 1024],
-                )
-            else:
-                nc.sync.dma_start(
-                    out=t[:, 0:2048].rearrange("p (g k) -> p g k", g=2),
-                    in_=Wg[g : g + 2].rearrange("g (q j) k -> q g j k", j=6)[:, :, j, :],
-                )
+            nc.sync.dma_start(
+                out=t[:, 0 : NJ * 1024],
+                in_=Wg[g].rearrange("(q j) k -> q (j k)", j=6)[:, j * 1024 : (j + NJ) * 1024],
+            )
             raw[m] = t
 
         chunks = ((0, 0), (1, 0), (0, 1), (1, 1))
@@ -159,43 +151,41 @@ def tile_groupwiselinearprojector_kernel(tc, x, Wg, bg, out):
                     in_=tb[:, 0 : len(js) * P].rearrange("p (j g) -> p j g", g=P)[:, :, 0:16],
                 )
 
-        ot = [keep.tile([P, 2048], F32, name="ot%d" % j) for j in range(6)]
         grp = {}
         codes = {}
-
         sorted_words = {}
+
+        def side_by_side(i):
+            a, b = pairs[i]
+            return a[0] == b[0] and a[3] + 512 == b[3]
+
+        def is_sorted(i):
+            return i > 3 and i % 3 == 0 and side_by_side(i)
 
         def sort_pair(i):
             st = srtp.tile([P, 2048], BF16, name="srt%d" % i, tag="srt", align_bytes=64)
-            units = pairs[i]
-            dst = st[:].bitcast(F32)
-            spans = [(units[0], 2)] if units[0][0] == units[1][0] and units[0][3] + 512 == units[1][3] else [(units[0], 1), (units[1], 1)]
-            at = 0
-            for (m, g, j, off), cnt in spans:
-                n = cnt * 512
-                nc.vector.tensor_copy(
-                    out=dst[:, at : at + n].rearrange("p (c u w) -> p c u w", u=2, w=P),
-                    in_=raw[m][:].bitcast(F32)[:, off : off + n].rearrange("p (c w u) -> p c u w", u=2, w=P),
-                )
-                at += n
-            sorted_words[i] = dst
+            m, g, j, off = pairs[i][0]
+            nc.vector.tensor_copy(
+                out=st[:].bitcast(F32).rearrange("p (c u w) -> p c u w", u=2, w=P),
+                in_=raw[m][:].bitcast(F32)[:, off : off + 1024].rearrange("p (c w u) -> p c u w", u=2, w=P),
+            )
+            sorted_words[i] = st
 
         def transpose_pair(i):
-            units = pairs[i]
             gt = grpp.tile([P, 2048], BF16, name="grp%d" % i, tag="grp", align_bytes=64)
             g32 = gt[:].bitcast(F32)
             banks = []
-            for n, (m, g, j, off) in enumerate(units):
-                if i in sorted_words:
-                    words, off = sorted_words[i], n * 512
-                else:
-                    words = raw[m][:].bitcast(F32)
+            for n, (m, g, j, off) in enumerate(pairs[i]):
                 tp = tps.tile([P, 512], F32, name="tp%d_%d" % (i, n), tag="tp")
                 for c in range(2):
                     for u in range(2):
                         s = 2 * c + u
-                        lo = off + 2 * P * c
-                        src = words[:, lo + u * P : lo + (u + 1) * P] if i in sorted_words else words[:, lo + u : lo + 2 * P : 2]
+                        if i in sorted_words:
+                            lo = n * 512 + s * P
+                            src = sorted_words[i][:].bitcast(F32)[:, lo : lo + P]
+                        else:
+                            lo = off + 2 * P * c
+                            src = raw[m][:].bitcast(F32)[:, lo + u : lo + 2 * P : 2]
                         nc.tensor.transpose(tp[:, s * P : (s + 1) * P], src, ident[:])
                 banks.append(tp)
             for n, tp in enumerate(banks):
@@ -231,7 +221,12 @@ def tile_groupwiselinearprojector_kernel(tc, x, Wg, bg, out):
                     )
             return po
 
+        ot = {}
+        done = [0] * 6
+
         def add_bias(pr, j, po):
+            if j not in ot:
+                ot[j] = outp.tile([P, 2048], F32, name="ot%d" % j, tag="ot")
             lo = 16 * j + 4 * pr
             nc.vector.tensor_tensor(
                 out=ot[j][:].rearrange("p (a r n) -> p r a n", a=16, r=4, n=32)[:, pr].rearrange("p a (w q) -> p a w q", q=4),
@@ -246,11 +241,7 @@ def tile_groupwiselinearprojector_kernel(tc, x, Wg, bg, out):
                     in_=ot[j][:].rearrange("p (b n) -> p b n", b=2),
                 )
 
-        done = [0] * 6
         x_stage()
-        def is_sorted(i):
-            return i % 2 == 0
-
         next_m = 0
         pending = []
         for i in range(n_pairs + LOOK + 1):

@@ -13,10 +13,9 @@ FLOPS = 2 * 16 * 128 * 1024 * 768
 
 P = 128
 LOOK = 3
-RAW_BUFS = 14
+RAW_BUFS = 12
 RAW_COLS = 4096
-NJ = 3
-SPACING = 2
+SPACING = 3
 
 
 def tile_groupwiselinearprojector_kernel(tc, x, Wg, bg, out):
@@ -25,9 +24,9 @@ def tile_groupwiselinearprojector_kernel(tc, x, Wg, bg, out):
         keep = ctx.enter_context(tc.tile_pool(name="keep", bufs=1))
         rawp = ctx.enter_context(tc.tile_pool(name="rawp", bufs=RAW_BUFS))
         grpp = ctx.enter_context(tc.tile_pool(name="grpp", bufs=5))
-        codp = ctx.enter_context(tc.tile_pool(name="codp", bufs=11))
-        srtp = ctx.enter_context(tc.tile_pool(name="srtp", bufs=2))
-        outp = ctx.enter_context(tc.tile_pool(name="outp", bufs=4))
+        codp = ctx.enter_context(tc.tile_pool(name="codp", bufs=10))
+        srtp = ctx.enter_context(tc.tile_pool(name="srtp", bufs=4))
+        outp = ctx.enter_context(tc.tile_pool(name="outp", bufs=6))
         tps = ctx.enter_context(tc.psum_pool(name="tps", bufs=6))
         pos = ctx.enter_context(tc.psum_pool(name="pos", bufs=2))
         ctx.enter_context(tc.manual_schedule())
@@ -39,16 +38,19 @@ def tile_groupwiselinearprojector_kernel(tc, x, Wg, bg, out):
         nc.vector.memset(bgpad[:], 0.0)
         nc.scalar.dma_start(out=bgpad[0:16, :], in_=bg)
 
-        tiles = [(g, 0) for g in range(16)] + [(g, NJ) for g in range(16)]
+        tiles = [[(0, 0), (0, 1)], [(0, 2), (0, 3)]]
+        tiles += [[(g, j) for j in range(4)] for g in range(1, 16)]
+        tiles += [[(g + a, 4 + b) for a in range(2) for b in range(2)] for g in range(0, 16, 2)]
+        place = {}
+        for m, units in enumerate(tiles):
+            for n, u in enumerate(units):
+                place[u] = (m, u[0], u[1], n * 512)
 
-        def unit(g, j):
-            return (g + 16 * (j // NJ), g, j, (j % NJ) * 512)
-
-        stream = [unit(g, j) for g in range(16) for j in (0, 1, 2)]
-        stream += [unit(g, j) for g in range(8) for j in (3, 4, 5)]
-        stream += [unit(g, j) for g in range(8, 16) for j in (3, 4)]
-        stream += [unit(g, 5) for g in range(8, 16)]
-        pairs = [(stream[n], stream[n + 1]) for n in range(0, len(stream), 2)]
+        stream = [(g, j) for g in range(16) for j in range(4)]
+        stream += [(g, j) for g in range(8) for j in (4, 5)]
+        stream += [(g, 4) for g in range(8, 16)]
+        stream += [(g, 5) for g in range(8, 16)]
+        pairs = [(place[stream[n]], place[stream[n + 1]]) for n in range(0, len(stream), 2)]
         n_pairs = len(pairs)
         where = {}
         last_pair = [0] * len(tiles)
@@ -57,27 +59,36 @@ def tile_groupwiselinearprojector_kernel(tc, x, Wg, bg, out):
                 where[(g, j)] = i
                 last_pair[m] = max(last_pair[m], i)
         order = sorted([(max([where[(4 * pr + q, j)] for q in range(4)]), j, pr) for pr in range(4) for j in range(6)])
+        bunches = [order[n : n + 2] for n in range(0, 22, 2)] + [order[22:23], order[23:24]]
+        avail = [max([av for av, j, pr in bunch]) for bunch in bunches]
         slots = []
-        for av, j, pr in order:
+        for av in avail:
             slots.append(max(av, slots[-1] + SPACING) if slots else av)
         lim = n_pairs - 1
-        for n in reversed(range(len(order))):
+        for n in reversed(range(len(bunches))):
             if slots[n] > lim:
-                slots[n] = max(order[n][0], lim)
+                slots[n] = max(avail[n], lim)
             lim = min(lim, slots[n]) - 1
         sched = [[] for k in range(n_pairs)]
-        for n, (av, j, pr) in enumerate(order):
-            sched[slots[n]].append((pr, j))
+        for n, bunch in enumerate(bunches):
+            sched[slots[n]] += [(pr, j) for av, j, pr in bunch]
 
         raw = {}
 
         def load_w(m):
-            g, j = tiles[m]
+            g, j = tiles[m][0]
+            n = len(tiles[m])
             t = rawp.tile([P, RAW_COLS], BF16, name="wr%d" % m, tag="raw", align_bytes=64)
-            nc.sync.dma_start(
-                out=t[:, 0 : NJ * 1024],
-                in_=Wg[g].rearrange("(q j) k -> q (j k)", j=6)[:, j * 1024 : (j + NJ) * 1024],
-            )
+            if tiles[m][-1][0] == g:
+                nc.sync.dma_start(
+                    out=t[:, 0 : n * 1024],
+                    in_=Wg[g].rearrange("(q j) k -> q (j k)", j=6)[:, j * 1024 : (j + n) * 1024],
+                )
+            else:
+                nc.sync.dma_start(
+                    out=t[:].rearrange("p (g n) -> p g n", g=2),
+                    in_=Wg[g : g + 2].rearrange("g (q j) k -> q g (j k)", j=6)[:, :, j * 1024 : (j + 2) * 1024],
+                )
             raw[m] = t
 
         chunks = ((0, 0), (1, 0), (0, 1), (1, 1))
@@ -155,19 +166,20 @@ def tile_groupwiselinearprojector_kernel(tc, x, Wg, bg, out):
         codes = {}
         sorted_words = {}
 
-        def side_by_side(i):
-            a, b = pairs[i]
-            return a[0] == b[0] and a[3] + 512 == b[3]
+        def by_vector(i):
+            return 16 <= i < n_pairs and i % 2 == 0
 
-        def is_sorted(i):
-            return i > 3 and i % 3 == 0 and side_by_side(i)
+        def by_scalar(i):
+            return 16 <= i < n_pairs and i % 8 == 1
 
-        def sort_pair(i):
+        def sort_pair(i, copy):
             st = srtp.tile([P, 2048], BF16, name="srt%d" % i, tag="srt", align_bytes=64)
-            m, g, j, off = pairs[i][0]
-            nc.vector.tensor_copy(
-                out=st[:].bitcast(F32).rearrange("p (c u w) -> p c u w", u=2, w=P),
-                in_=raw[m][:].bitcast(F32)[:, off : off + 1024].rearrange("p (c w u) -> p c u w", u=2, w=P),
+            m = pairs[i][0][0]
+            a, b = [off // 512 for mm, g, j, off in pairs[i]]
+            src = raw[m][:].bitcast(F32).rearrange("p (n c w u) -> p n c u w", n=4, c=2, u=2)
+            copy(
+                out=st[:].bitcast(F32).rearrange("p (n c u w) -> p n c u w", n=2, c=2, u=2),
+                in_=src[:, a : b + 1 : b - a],
             )
             sorted_words[i] = st
 
@@ -228,18 +240,22 @@ def tile_groupwiselinearprojector_kernel(tc, x, Wg, bg, out):
             if j not in ot:
                 ot[j] = outp.tile([P, 2048], F32, name="ot%d" % j, tag="ot")
             lo = 16 * j + 4 * pr
-            nc.vector.tensor_tensor(
-                out=ot[j][:].rearrange("p (a r n) -> p r a n", a=16, r=4, n=32)[:, pr].rearrange("p a (w q) -> p a w q", q=4),
-                in0=po[:].rearrange("p (q a w) -> p a w q", q=4, a=16, w=8),
-                in1=bias[:, lo : lo + 4].unsqueeze(1).unsqueeze(1).to_broadcast([P, 16, 8, 4]),
-                op=mybir.AluOpType.add,
-            )
             done[j] += 1
-            if done[j] == 4:
-                nc.sync.dma_start(
-                    out=out.rearrange("b (q j) h w -> j q b (h w)", j=6)[j],
-                    in_=ot[j][:].rearrange("p (b n) -> p b n", b=2),
+            parts = ((0, 1), (1, 2)) if done == [4] * 6 else ((0, 2),)
+            for b0, b1 in parts:
+                nb = b1 - b0
+                dst = ot[j][:].rearrange("p (a r n) -> p r a n", a=16, r=4, n=32)[:, pr, 8 * b0 : 8 * b1]
+                nc.vector.tensor_tensor(
+                    out=dst.rearrange("p a (w q) -> p a w q", q=4),
+                    in0=po[:].rearrange("p (q a w) -> p a w q", q=4, a=16, w=8)[:, 8 * b0 : 8 * b1],
+                    in1=bias[:, lo : lo + 4].unsqueeze(1).unsqueeze(1).to_broadcast([P, 8 * nb, 8, 4]),
+                    op=mybir.AluOpType.add,
                 )
+                if done[j] == 4:
+                    nc.sync.dma_start(
+                        out=out.rearrange("b (q j) h w -> j q b (h w)", j=6)[j][:, b0:b1],
+                        in_=ot[j][:].rearrange("p (b n) -> p b n", b=2)[:, b0:b1],
+                    )
 
         x_stage()
         next_m = 0
@@ -253,8 +269,10 @@ def tile_groupwiselinearprojector_kernel(tc, x, Wg, bg, out):
             if i < n_pairs:
                 transpose_pair(i)
             k = i - LOOK
-            if i + 2 < n_pairs and is_sorted(i + 2):
-                sort_pair(i + 2)
+            if by_vector(i + 2):
+                sort_pair(i + 2, nc.vector.tensor_copy)
+            if by_scalar(i + 4):
+                sort_pair(i + 4, nc.scalar.copy)
             if 0 <= k < n_pairs:
                 quant_pair(k)
             for pr, j, po in pending:

@@ -15,7 +15,7 @@ P = 128
 LOOK = 3
 RAW_BUFS = 12
 RAW_COLS = 4096
-SPACING = 3
+SPACING = 2
 
 
 def tile_groupwiselinearprojector_kernel(tc, x, Wg, bg, out):
@@ -24,8 +24,8 @@ def tile_groupwiselinearprojector_kernel(tc, x, Wg, bg, out):
         keep = ctx.enter_context(tc.tile_pool(name="keep", bufs=1))
         rawp = ctx.enter_context(tc.tile_pool(name="rawp", bufs=RAW_BUFS))
         grpp = ctx.enter_context(tc.tile_pool(name="grpp", bufs=5))
-        codp = ctx.enter_context(tc.tile_pool(name="codp", bufs=10))
-        srtp = ctx.enter_context(tc.tile_pool(name="srtp", bufs=4))
+        codp = ctx.enter_context(tc.tile_pool(name="codp", bufs=12))
+        srtp = ctx.enter_context(tc.tile_pool(name="srtp", bufs=2))
         outp = ctx.enter_context(tc.tile_pool(name="outp", bufs=6))
         tps = ctx.enter_context(tc.psum_pool(name="tps", bufs=6))
         pos = ctx.enter_context(tc.psum_pool(name="pos", bufs=2))
@@ -59,7 +59,7 @@ def tile_groupwiselinearprojector_kernel(tc, x, Wg, bg, out):
                 where[(g, j)] = i
                 last_pair[m] = max(last_pair[m], i)
         order = sorted([(max([where[(4 * pr + q, j)] for q in range(4)]), j, pr) for pr in range(4) for j in range(6)])
-        bunches = [order[n : n + 2] for n in range(0, 22, 2)] + [order[22:23], order[23:24]]
+        bunches = [[o] for o in order]
         avail = [max([av for av, j, pr in bunch]) for bunch in bunches]
         slots = []
         for av in avail:
@@ -110,19 +110,18 @@ def tile_groupwiselinearprojector_kernel(tc, x, Wg, bg, out):
                 src = (
                     xr[(b, c)][:, 0:4096]
                     .rearrange("p (a r n) -> p r a n", a=32, r=4, n=32)[:, pr]
-                    .rearrange("p (t h) (w q) -> p q h w t", t=4, q=4)
+                    .rearrange("p (t h) (w q) -> p h w q t", t=4, q=4)
                 )
                 lo = (pr % 2) * 2048
                 dst = (
                     gx[(c, pr // 2)][:, lo : lo + 2048]
                     .rearrange("p (q b n) -> p q b n", q=4, b=2)[:, :, b]
-                    .rearrange("p q (h w t) -> p q h w t", h=8, w=8, t=4)
+                    .rearrange("p q (h w t) -> p h w q t", h=8, w=8, t=4)
                 )
                 if pr < 3:
                     nc.vector.tensor_copy(out=dst, in_=src)
                 else:
-                    for q in range(4):
-                        nc.scalar.copy(out=dst[:, q], in_=src[:, q])
+                    nc.scalar.copy(out=dst, in_=src)
 
         def quant_x(c, gh):
             base = (c * 16 + gh * 8) * P
@@ -168,9 +167,6 @@ def tile_groupwiselinearprojector_kernel(tc, x, Wg, bg, out):
 
         def by_vector(i):
             return 16 <= i < n_pairs and i % 2 == 0
-
-        def by_scalar(i):
-            return 16 <= i < n_pairs and i % 8 == 1
 
         def sort_pair(i, copy):
             st = srtp.tile([P, 2048], BF16, name="srt%d" % i, tag="srt", align_bytes=64)
@@ -271,8 +267,6 @@ def tile_groupwiselinearprojector_kernel(tc, x, Wg, bg, out):
             k = i - LOOK
             if by_vector(i + 2):
                 sort_pair(i + 2, nc.vector.tensor_copy)
-            if by_scalar(i + 4):
-                sort_pair(i + 4, nc.scalar.copy)
             if 0 <= k < n_pairs:
                 quant_pair(k)
             for pr, j, po in pending:

@@ -110,13 +110,13 @@ def tile_groupwiselinearprojector_kernel(tc, x, Wg, bg, out):
                 src = (
                     xr[(b, c)][:, 0:4096]
                     .rearrange("p (a r n) -> p r a n", a=32, r=4, n=32)[:, pr]
-                    .rearrange("p (t h) (w q) -> p h w q t", t=4, q=4)
+                    .rearrange("p (t h) (w q) -> p h w t q", t=4, q=4)
                 )
                 lo = (pr % 2) * 2048
                 dst = (
                     gx[(c, pr // 2)][:, lo : lo + 2048]
                     .rearrange("p (q b n) -> p q b n", q=4, b=2)[:, :, b]
-                    .rearrange("p q (h w t) -> p h w q t", h=8, w=8, t=4)
+                    .rearrange("p q (h w t) -> p h w t q", h=8, w=8, t=4)
                 )
                 if pr < 3:
                     nc.vector.tensor_copy(out=dst, in_=src)
@@ -269,9 +269,10 @@ def tile_groupwiselinearprojector_kernel(tc, x, Wg, bg, out):
                 sort_pair(i + 2, nc.vector.tensor_copy)
             if 0 <= k < n_pairs:
                 quant_pair(k)
-            for pr, j, po in pending:
+            ready = [p for p in pending if p[0] <= i - 2 or i > n_pairs]
+            pending = [p for p in pending if p not in ready]
+            for at, pr, j, po in ready:
                 add_bias(pr, j, po)
-            pending = []
             if 0 <= k < n_pairs:
                 for pr, j in sched[k]:
-                    pending.append((pr, j, multiply(pr, j)))
+                    pending.append((i, pr, j, multiply(pr, j)))

@@ -118,7 +118,7 @@ def tile_groupwiselinearprojector_kernel(tc, x, Wg, bg, out):
                     .rearrange("p (q b n) -> p q b n", q=4, b=2)[:, :, b]
                     .rearrange("p q (h w t) -> p h w t q", h=8, w=8, t=4)
                 )
-                if pr < 3:
+                if pr < (3 if (b, c) == chunks[-1] else 2):
                     nc.vector.tensor_copy(out=dst, in_=src)
                 else:
                     nc.scalar.copy(out=dst, in_=src)
@@ -166,7 +166,7 @@ def tile_groupwiselinearprojector_kernel(tc, x, Wg, bg, out):
         sorted_words = {}
 
         def by_vector(i):
-            return 16 <= i < n_pairs and i % 2 == 0
+            return 15 <= i < n_pairs and i % 3 == 0
 
         def sort_pair(i, copy):
             st = srtp.tile([P, 2048], BF16, name="srt%d" % i, tag="srt", align_bytes=64)

@@ -36,9 +36,8 @@ def tile_groupwiselinearprojector_kernel(tc, x, Wg, bg, out):
 
         bgpad = keep.tile([P, 768], BF16, name="bgpad")
         nc.vector.memset(bgpad[:], 0.0)
-        nc.scalar.dma_start(out=bgpad[0:16, :], in_=bg)
 
-        tiles = [[(0, 0), (0, 1)], [(0, 2), (0, 3)]]
+        tiles = [[(0, 0)], [(0, 1)], [(0, 2), (0, 3)]]
         tiles += [[(g, j) for j in range(4)] for g in range(1, 16)]
         tiles += [[(g + a, 4 + b) for a in range(2) for b in range(2)] for g in range(0, 16, 2)]
         place = {}
@@ -100,6 +99,8 @@ def tile_groupwiselinearprojector_kernel(tc, x, Wg, bg, out):
                 in_=x[b, 512 * c : 512 * c + 512].rearrange("(p t) h w -> p (t h w)", t=4),
             )
             xr[(b, c)] = t
+            if (b, c) == chunks[0]:
+                nc.sync.dma_start(out=bgpad[0:16, :], in_=bg)
 
         xc = keep.tile([P, 4096], U32, name="xc", align_bytes=64)
         xs = keep.tile([P, 4096], U8, name="xs", align_bytes=64)
@@ -139,17 +140,18 @@ def tile_groupwiselinearprojector_kernel(tc, x, Wg, bg, out):
                 for gh in range(2):
                     gx[(c, gh)] = rawp.tile([P, RAW_COLS], BF16, name="gx%d%d" % (c, gh), tag="raw", align_bytes=64)
             regroup(0, 0)
+            nc.vector.tensor_copy(
+                out=bgf[:].rearrange("g (j q) -> g j q", j=6),
+                in_=bgpad[:].rearrange("g (q j) -> g j q", j=6),
+            )
             regroup(1, 0)
+            spread_bias()
             regroup(0, 1)
             quant_x(0, 0)
             quant_x(0, 1)
             regroup(1, 1)
             quant_x(1, 0)
             quant_x(1, 1)
-            nc.vector.tensor_copy(
-                out=bgf[:].rearrange("g (j q) -> g j q", j=6),
-                in_=bgpad[:].rearrange("g (q j) -> g j q", j=6),
-            )
 
         def spread_bias():
             for js in ((0, 1, 2, 3), (4, 5)):
@@ -166,7 +168,7 @@ def tile_groupwiselinearprojector_kernel(tc, x, Wg, bg, out):
         sorted_words = {}
 
         def by_vector(i):
-            return 15 <= i < n_pairs and i % 3 == 0
+            return 15 <= i < n_pairs and i % 5 in (0, 2)
 
         def sort_pair(i, copy):
             st = srtp.tile([P, 2048], BF16, name="srt%d" % i, tag="srt", align_bytes=64)
@@ -237,20 +239,25 @@ def tile_groupwiselinearprojector_kernel(tc, x, Wg, bg, out):
                 ot[j] = outp.tile([P, 2048], F32, name="ot%d" % j, tag="ot")
             lo = 16 * j + 4 * pr
             done[j] += 1
-            parts = ((0, 1), (1, 2)) if done == [4] * 6 else ((0, 2),)
-            for b0, b1 in parts:
-                nb = b1 - b0
-                dst = ot[j][:].rearrange("p (a r n) -> p r a n", a=16, r=4, n=32)[:, pr, 8 * b0 : 8 * b1]
+            n_parts = 4 if done == [4] * 6 else 1
+            na = 16 // n_parts
+            for a0 in range(0, 16, na):
+                dst = ot[j][:].rearrange("p (a r n) -> p r a n", a=16, r=4, n=32)[:, pr, a0 : a0 + na]
                 nc.vector.tensor_tensor(
                     out=dst.rearrange("p a (w q) -> p a w q", q=4),
-                    in0=po[:].rearrange("p (q a w) -> p a w q", q=4, a=16, w=8)[:, 8 * b0 : 8 * b1],
-                    in1=bias[:, lo : lo + 4].unsqueeze(1).unsqueeze(1).to_broadcast([P, 8 * nb, 8, 4]),
+                    in0=po[:].rearrange("p (q a w) -> p a w q", q=4, a=16, w=8)[:, a0 : a0 + na],
+                    in1=bias[:, lo : lo + 4].unsqueeze(1).unsqueeze(1).to_broadcast([P, na, 8, 4]),
                     op=mybir.AluOpType.add,
                 )
-                if done[j] == 4:
+                if done[j] == 4 and n_parts == 1:
                     nc.sync.dma_start(
-                        out=out.rearrange("b (q j) h w -> j q b (h w)", j=6)[j][:, b0:b1],
-                        in_=ot[j][:].rearrange("p (b n) -> p b n", b=2)[:, b0:b1],
+                        out=out.rearrange("b (q j) h w -> j q b (h w)", j=6)[j],
+                        in_=ot[j][:].rearrange("p (b n) -> p b n", b=2),
+                    )
+                elif done[j] == 4:
+                    nc.sync.dma_start(
+                        out=out.rearrange("b (q j) (s h) w -> j b s q (h w)", j=6, s=2)[j, a0 // 8, a0 // na % 2],
+                        in_=ot[j][:, a0 * 128 : (a0 + na) * 128],
                     )
 
         x_stage()
@@ -260,8 +267,6 @@ def tile_groupwiselinearprojector_kernel(tc, x, Wg, bg, out):
             while next_m < len(tiles) and (next_m < RAW_BUFS or last_pair[next_m - RAW_BUFS] < i):
                 load_w(next_m)
                 next_m += 1
-            if i == 8:
-                spread_bias()
             if i < n_pairs:
                 transpose_pair(i)
             k = i - LOOK

@@ -168,7 +168,7 @@ def tile_groupwiselinearprojector_kernel(tc, x, Wg, bg, out):
         sorted_words = {}
 
         def by_vector(i):
-            return 15 <= i < n_pairs and i % 5 in (0, 2)
+            return 16 <= i < n_pairs and i % 2 == 0
 
         def sort_pair(i, copy):
             st = srtp.tile([P, 2048], BF16, name="srt%d" % i, tag="srt", align_bytes=64)
@@ -270,14 +270,14 @@ def tile_groupwiselinearprojector_kernel(tc, x, Wg, bg, out):
             if i < n_pairs:
                 transpose_pair(i)
             k = i - LOOK
-            if by_vector(i + 2):
-                sort_pair(i + 2, nc.vector.tensor_copy)
             if 0 <= k < n_pairs:
                 quant_pair(k)
             ready = [p for p in pending if p[0] <= i - 2 or i > n_pairs]
             pending = [p for p in pending if p not in ready]
             for at, pr, j, po in ready:
                 add_bias(pr, j, po)
+            if by_vector(i + 2):
+                sort_pair(i + 2, nc.vector.tensor_copy)
             if 0 <= k < n_pairs:
                 for pr, j in sched[k]:
                     pending.append((i, pr, j, multiply(pr, j)))

from contextlib import ExitStack

import concourse.mybir as mybir
from concourse.masks import make_identity

F32 = mybir.dt.float32
BF16 = mybir.dt.bfloat16
U32 = mybir.dt.uint32
U8 = mybir.dt.uint8
FP8X4 = mybir.dt.float8_e4m3fn_x4

FLOPS = 2 * 16 * 128 * 1024 * 768

P = 128
LOOK = 3
RAW_BUFS = 12
RAW_COLS = 4096
SPACING = 2


def tile_groupwiselinearprojector_kernel(tc, x, Wg, bg, out):
    nc = tc.nc
    with ExitStack() as ctx:
        keep = ctx.enter_context(tc.tile_pool(name="keep", bufs=1))
        rawp = ctx.enter_context(tc.tile_pool(name="rawp", bufs=RAW_BUFS))
        grpp = ctx.enter_context(tc.tile_pool(name="grpp", bufs=5))
        codp = ctx.enter_context(tc.tile_pool(name="codp", bufs=12))
        srtp = ctx.enter_context(tc.tile_pool(name="srtp", bufs=2))
        outp = ctx.enter_context(tc.tile_pool(name="outp", bufs=6))
        tps = ctx.enter_context(tc.psum_pool(name="tps", bufs=6))
        pos = ctx.enter_context(tc.psum_pool(name="pos", bufs=2))
        ctx.enter_context(tc.manual_schedule())

        ident = keep.tile([P, P], F32, name="ident")
        make_identity(nc, ident[:])

        bgpad = keep.tile([P, 768], BF16, name="bgpad")
        nc.vector.memset(bgpad[:], 0.0)

        tiles = [[(0, 0)], [(0, 1)], [(0, 2), (0, 3)]]
        tiles += [[(g, j) for j in range(4)] for g in range(1, 16)]
        tiles += [[(g + a, 4 + b) for a in range(2) for b in range(2)] for g in range(0, 16, 2)]
        place = {}
        for m, units in enumerate(tiles):
            for n, u in enumerate(units):
                place[u] = (m, u[0], u[1], n * 512)

        stream = [(g, j) for g in range(16) for j in range(4)]
        stream += [(g, j) for g in range(8) for j in (4, 5)]
        stream += [(g, 4) for g in range(8, 16)]
        stream += [(g, 5) for g in range(8, 16)]
        pairs = [(place[stream[n]], place[stream[n + 1]]) for n in range(0, len(stream), 2)]
        n_pairs = len(pairs)
        where = {}
        last_pair = [0] * len(tiles)
        for i, units in enumerate(pairs):
            for m, g, j, off in units:
                where[(g, j)] = i
                last_pair[m] = max(last_pair[m], i)
        order = sorted([(max([where[(4 * pr + q, j)] for q in range(4)]), j, pr) for pr in range(4) for j in range(6)])
        bunches = [[o] for o in order]
        avail = [max([av for av, j, pr in bunch]) for bunch in bunches]
        slots = []
        for av in avail:
            slots.append(max(av, slots[-1] + SPACING) if slots else av)
        lim = n_pairs - 1
        for n in reversed(range(len(bunches))):
            if slots[n] > lim:
                slots[n] = max(avail[n], lim)
            lim = min(lim, slots[n]) - 1
        sched = [[] for k in range(n_pairs)]
        for n, bunch in enumerate(bunches):
            sched[slots[n]] += [(pr, j) for av, j, pr in bunch]

        raw = {}

        def load_w(m):
            g, j = tiles[m][0]
            n = len(tiles[m])
            t = rawp.tile([P, RAW_COLS], BF16, name="wr%d" % m, tag="raw", align_bytes=64)
            if tiles[m][-1][0] == g:
                nc.sync.dma_start(
                    out=t[:, 0 : n * 1024],
                    in_=Wg[g].rearrange("(q j) k -> q (j k)", j=6)[:, j * 1024 : (j + n) * 1024],
                )
            else:
                nc.sync.dma_start(
                    out=t[:].rearrange("p (g n) -> p g n", g=2),
                    in_=Wg[g : g + 2].rearrange("g (q j) k -> q g (j k)", j=6)[:, :, j * 1024 : (j + 2) * 1024],
                )
            raw[m] = t

        chunks = ((0, 0), (1, 0), (0, 1), (1, 1))
        xr = {}
        for b, c in chunks:
            t = rawp.tile([P, RAW_COLS], BF16, name="xr%d%d" % (b, c), tag="raw", align_bytes=64)
            nc.sync.dma_start(
                out=t[:, 0:4096],
                in_=x[b, 512 * c : 512 * c + 512].rearrange("(p t) h w -> p (t h w)", t=4),
            )
            xr[(b, c)] = t
            if (b, c) == chunks[0]:
                nc.sync.dma_start(out=bgpad[0:16, :], in_=bg)

        xc = keep.tile([P, 4096], U32, name="xc", align_bytes=64)
        xs = keep.tile([P, 4096], U8, name="xs", align_bytes=64)
        gx = {}

        def regroup(b, c):
            for pr in range(4):
                src = (
                    xr[(b, c)][:, 0:4096]
                    .rearrange("p (a r n) -> p r a n", a=32, r=4, n=32)[:, pr]
                    .rearrange("p (t h) (w q) -> p h w t q", t=4, q=4)
                )
                lo = (pr % 2) * 2048
                dst = (
                    gx[(c, pr // 2)][:, lo : lo + 2048]
                    .rearrange("p (q b n) -> p q b n", q=4, b=2)[:, :, b]
                    .rearrange("p q (h w t) -> p h w t q", h=8, w=8, t=4)
                )
                if pr < (3 if (b, c) == chunks[-1] else 2):
                    nc.vector.tensor_copy(out=dst, in_=src)
                else:
                    nc.scalar.copy(out=dst, in_=src)

        def quant_x(c, gh):
            base = (c * 16 + gh * 8) * P
            nc.vector.quantize_mx(
                out=xc[:, base : base + 1024].bitcast(FP8X4),
                scales=xs[:, base : base + 1024],
                in_=gx[(c, gh)][:, 0:4096],
            )

        bgf = keep.tile([P, 768], F32, name="bgf")
        bias = keep.tile([P, 96], F32, name="bias")

        def x_stage():
            for c in range(2):
                for gh in range(2):
                    gx[(c, gh)] = rawp.tile([P, RAW_COLS], BF16, name="gx%d%d" % (c, gh), tag="raw", align_bytes=64)
            regroup(0, 0)
            nc.vector.tensor_copy(
                out=bgf[:].rearrange("g (j q) -> g j q", j=6),
                in_=bgpad[:].rearrange("g (q j) -> g j q", j=6),
            )
            regroup(1, 0)
            spread_bias()
            regroup(0, 1)
            quant_x(0, 0)
            quant_x(0, 1)
            regroup(1, 1)
            quant_x(1, 0)
            quant_x(1, 1)

        def spread_bias():
            for js in ((0, 1, 2, 3), (4, 5)):
                tb = tps.tile([P, 512], F32, name="tb%d" % js[0], tag="tp")
                for n, j in enumerate(js):
                    nc.tensor.transpose(tb[:, n * P : (n + 1) * P], bgf[:, j * P : (j + 1) * P], ident[:])
                nc.scalar.copy(
                    out=bias[:, js[0] * 16 : (js[-1] + 1) * 16].rearrange("p (j g) -> p j g", g=16),
                    in_=tb[:, 0 : len(js) * P].rearrange("p (j g) -> p j g", g=P)[:, :, 0:16],
                )

        grp = {}
        codes = {}
        sorted_words = {}

        def by_vector(i):
            return 16 <= i < n_pairs and i % 2 == 0

        def sort_pair(i, copy):
            st = srtp.tile([P, 2048], BF16, name="srt%d" % i, tag="srt", align_bytes=64)
            m = pairs[i][0][0]
            a, b = [off // 512 for mm, g, j, off in pairs[i]]
            src = raw[m][:].bitcast(F32).rearrange("p (n c w u) -> p n c u w", n=4, c=2, u=2)
            copy(
                out=st[:].bitcast(F32).rearrange("p (n c u w) -> p n c u w", n=2, c=2, u=2),
                in_=src[:, a : b + 1 : b - a],
            )
            sorted_words[i] = st

        def transpose_pair(i):
            gt = grpp.tile([P, 2048], BF16, name="grp%d" % i, tag="grp", align_bytes=64)
            g32 = gt[:].bitcast(F32)
            banks = []
            for n, (m, g, j, off) in enumerate(pairs[i]):
                tp = tps.tile([P, 512], F32, name="tp%d_%d" % (i, n), tag="tp")
                for c in range(2):
                    for u in range(2):
                        s = 2 * c + u
                        if i in sorted_words:
                            lo = n * 512 + s * P
                            src = sorted_words[i][:].bitcast(F32)[:, lo : lo + P]
                        else:
                            lo = off + 2 * P * c
                            src = raw[m][:].bitcast(F32)[:, lo + u : lo + 2 * P : 2]
                        nc.tensor.transpose(tp[:, s * P : (s + 1) * P], src, ident[:])
                banks.append(tp)
            for n, tp in enumerate(banks):
                nc.scalar.copy(
                    out=g32[:, n * 512 : (n + 1) * 512].rearrange("p (c o u) -> p c o u", c=2, o=P, u=2),
                    in_=tp[:].rearrange("p (c u o) -> p c o u", c=2, u=2, o=P),
                )
            grp[i] = gt

        def quant_pair(i):
            wc = codp.tile([P, 512], U32, name="wc%d" % i, tag="wc", align_bytes=64)
            ws = codp.tile([P, 512], U8, name="ws%d" % i, tag="ws", align_bytes=64)
            nc.vector.quantize_mx(out=wc[:].bitcast(FP8X4), scales=ws[:], in_=grp[i][:])
            for n, (m, g, j, off) in enumerate(pairs[i]):
                codes[(g, j)] = (wc, ws, n)

        def multiply(pr, j):
            po = pos.tile([P, 512], F32, name="po%d_%d" % (pr, j), tag="po")
            for q in range(4):
                g = 4 * pr + q
                wc, ws, n = codes[(g, j)]
                for c in range(2):
                    wl = (2 * n + c) * P
                    xl = (16 * c + g) * P
                    nc.tensor.matmul_mx(
                        out=po[:, q * P : (q + 1) * P],
                        lhsT=wc[:, wl : wl + P].bitcast(FP8X4),
                        lhsT_scale=ws[:, wl : wl + P],
                        rhs=xc[:, xl : xl + P].bitcast(FP8X4),
                        rhs_scale=xs[:, xl : xl + P],
                        start=(c == 0),
                        stop=(c == 1),
                    )
            return po

        ot = {}
        done = [0] * 6

        def add_bias(pr, j, po):
            if j not in ot:
                ot[j] = outp.tile([P, 2048], F32, name="ot%d" % j, tag="ot")
            lo = 16 * j + 4 * pr
            done[j] += 1
            n_parts = 4 if done == [4] * 6 else 1
            na = 16 // n_parts
            for a0 in range(0, 16, na):
                dst = ot[j][:].rearrange("p (a r n) -> p r a n", a=16, r=4, n=32)[:, pr, a0 : a0 + na]
                nc.vector.tensor_tensor(
                    out=dst.rearrange("p a (w q) -> p a w q", q=4),
                    in0=po[:].rearrange("p (q a w) -> p a w q", q=4, a=16, w=8)[:, a0 : a0 + na],
                    in1=bias[:, lo : lo + 4].unsqueeze(1).unsqueeze(1).to_broadcast([P, na, 8, 4]),
                    op=mybir.AluOpType.add,
                )
                if done[j] == 4 and n_parts == 1:
                    nc.sync.dma_start(
                        out=out.rearrange("b (q j) h w -> j q b (h w)", j=6)[j],
                        in_=ot[j][:].rearrange("p (b n) -> p b n", b=2),
                    )
                elif done[j] == 4:
                    nc.sync.dma_start(
                        out=out.rearrange("b (q j) (s h) w -> j b s q (h w)", j=6, s=2)[j, a0 // 8, a0 // na % 2],
                        in_=ot[j][:, a0 * 128 : (a0 + na) * 128],
                    )

        x_stage()
        next_m = 0
        pending = []
        for i in range(n_pairs + LOOK + 1):
            while next_m < len(tiles) and (next_m < RAW_BUFS or last_pair[next_m - RAW_BUFS] < i):
                load_w(next_m)
                next_m += 1
            if i < n_pairs:
                transpose_pair(i)
            k = i - LOOK
            if 0 <= k < n_pairs:
                quant_pair(k)
            ready = [p for p in pending if p[0] <= i - 2 or i > n_pairs]
            pending = [p for p in pending if p not in ready]
            for at, pr, j, po in ready:
                add_bias(pr, j, po)
            if by_vector(i + 2):
                sort_pair(i + 2, nc.vector.tensor_copy)
            if 0 <= k < n_pairs:
                for pr, j in sched[k]:
                    pending.append((i, pr, j, multiply(pr, j)))
